import numpy as np
import ml_dtypes


def mxq(x, axis, fmt="e4m3"):
    dtype, down = {"e4m3": (ml_dtypes.float8_e4m3fn, 7), "e5m2": (ml_dtypes.float8_e5m2, 14)}[fmt]
    v = np.moveaxis(np.asarray(x, np.float32).astype(ml_dtypes.bfloat16).astype(np.float64), axis, -1)
    blocks = v.reshape(v.shape[:-1] + (-1, 32))
    amax = np.abs(blocks).max(-1, keepdims=True)
    byte = np.maximum(np.where(amax > 0, np.frexp(amax)[1] - 1 + 127, 0) - down, 1)
    scale = np.exp2(byte - 127.0)
    codes = (blocks / scale).astype(np.float32).astype(dtype).astype(np.float64)
    return np.moveaxis((codes * scale).reshape(v.shape), -1, axis)


WIDE = False


def mx_kscale(k):
    if not WIDE:
        return np.ones(k)
    levels = np.array([10, -10, 5, -5, 0])
    a = np.random.permutation(np.resize(levels, k // 512 * 4)).reshape(k // 512, 4)
    idx = np.arange(k)
    return np.exp2(a[idx // 512, idx % 128 // 32])


BF16 = ml_dtypes.bfloat16


def bf(x):
    return np.asarray(x, np.float32).astype(BF16)


def f64(x):
    return np.asarray(x).astype(np.float64)


B, P, L, K = 512, 8, 1024, 512
GAUSS_STD = 10.0
PER = 4 * 32


def setup_inputs():
    s = mx_kscale(L)
    r = float(s.max() / s.min())
    f = np.where((np.arange(L) // 32) % 4 == 0, r, 1.0)
    x = np.random.standard_normal((B, P, L)) * 0.5 * f
    u = np.random.random(K) * (L // PER)
    j = np.floor(u)
    weight = u * PER if r == 1.0 else PER * j + 68.0 + 24.0 * (u - j)
    return {"x": bf(x.reshape(B, P * L)), "weight": bf(weight)}


def reference(x, weight):
    t = np.arange(1, L + 1, dtype=np.float64)
    W = np.exp(-((t[:, None] - f64(weight)[None, :]) ** 2) / (GAUSS_STD ** 2))
    xb = f64(x).reshape(B, P, L)
    out = mxq(xb, 2, "e4m3") @ mxq(W, 0, "e4m3")
    return out.reshape(B, P * K)

@@ -1,0 +1,194 @@
+from contextlib import ExitStack
+
+import concourse.mybir as mybir
+from concourse.masks import make_identity
+
+F32 = mybir.dt.float32
+BF16 = mybir.dt.bfloat16
+I32 = mybir.dt.int32
+U32 = mybir.dt.uint32
+U8 = mybir.dt.uint8
+FP8X4 = mybir.dt.float8_e4m3fn_x4
+ACT = mybir.ActivationFunctionType
+
+P = 128
+ROWS = 4096
+L = 1024
+K = 512
+TILES = ROWS // P
+GROUP = 4
+FLOPS = 2 * ROWS * L * K
+
+LOADS = [1, 1, 2, 4, 4, 4, 4, 4, 4, 4]
+STORES = [4, 4, 4, 4, 4, 2, 2, 2, 2, 1, 1, 1, 1]
+
+
+def tile_samplinglayer_kernel(tc, x, weight, out):
+    nc = tc.nc
+    xv = x.rearrange("(p a) f -> p (a f)", p=P)
+    ov = out.rearrange("(p a) f -> p (a f)", p=P)
+
+    with ExitStack() as ctx:
+        const = ctx.enter_context(tc.tile_pool(name="const", bufs=1))
+        xpool = ctx.enter_context(tc.tile_pool(name="xpool", bufs=1))
+        gpool = ctx.enter_context(tc.tile_pool(name="gpool", bufs=4))
+        cpool = ctx.enter_context(tc.tile_pool(name="cpool", bufs=1))
+        opool = ctx.enter_context(tc.tile_pool(name="opool", bufs=3))
+        psum = ctx.enter_context(tc.psum_pool(name="psum", bufs=1))
+        ctx.enter_context(tc.manual_schedule())
+
+        nb_i = const.tile([P, 8], I32, name="nb_i")
+        nc.gpsimd.iota(nb_i[:], pattern=[[-512, 2], [-256, 2], [-1, 2]], base=-1, channel_multiplier=-2)
+        ident = const.tile([P, P], F32, name="ident")
+        make_identity(nc, ident[:])
+
+        zero1 = const.tile([P, 1], F32, name="zero1")
+        nc.vector.memset(zero1[:], 0.0)
+        wz = const.tile([P, K], BF16, name="wz")
+        nc.vector.memset(wz[0:64, :], 0.0)
+        nc.vector.memset(wz[64:96, :], 0.0)
+        nc.vector.memset(wz[96:127, :], 0.0)
+        ones = const.tile([P, P], BF16, name="ones")
+        nc.vector.memset(ones[:], 1.0)
+        nb = const.tile([P, 8], F32, name="nb")
+        nc.vector.tensor_copy(out=nb[:], in_=nb_i[:])
+
+        warm = const.tile([P, 1], F32, name="warm")
+        nc.scalar.activation(out=warm[:], in_=zero1[:], func=ACT.Exp)
+
+        nc.sync.dma_start(out=wz[127:128, :], in_=weight.rearrange("(o n) -> o n", o=1))
+        xw = {}
+        t0 = 0
+        for c, n in enumerate(LOADS):
+            xt = xpool.tile([P, n * L], BF16, name="x%d" % c)
+            nc.sync.dma_start(out=xt[:], in_=xv[:, t0 * L:(t0 + n) * L])
+            words = xt[:].bitcast(F32)
+            for i in range(n):
+                xw[t0 + i] = words[:, i * (L // 2):(i + 1) * (L // 2)]
+            t0 += n
+
+        wbc = psum.tile([P, K], F32, tag="po3", name="wbc")
+        nc.tensor.matmul(out=wbc[:], lhsT=ones[:], rhs=wz[:], start=True, stop=True)
+        sq = const.tile([P, 8 * K], F32, name="sq")
+        for j in range(8):
+            nc.scalar.activation(out=sq[:, j * K:(j + 1) * K], in_=wbc[:], func=ACT.Square,
+                                 bias=nb[:, j:j + 1], scale=1.0)
+        wg = []
+        wcodes = []
+        wscl = []
+        for g in range(2):
+            wg_g = const.tile([P, 4 * K], BF16, name="wg%d" % g, align_bytes=64)
+            nc.scalar.activation(out=wg_g[:].rearrange("p (n t) -> p n t", t=4),
+                                 in_=sq[:, g * 4 * K:(g + 1) * 4 * K].rearrange("p (t n) -> p n t", t=4),
+                                 func=ACT.Exp, scale=-0.01)
+            wg.append(wg_g)
+            wc_g = const.tile([P, K], U32, name="wcodes%d" % g, align_bytes=64)
+            ws_g = const.tile([P, K], U8, name="wscl%d" % g, align_bytes=64)
+            wcodes.append(wc_g)
+            wscl.append(ws_g)
+
+        def quantise_w(g):
+            nc.vector.quantize_mx(out=wcodes[g][:].bitcast(FP8X4), scales=wscl[g][:], in_=wg[g][:])
+
+        pt = {}
+        po = {}
+        grouped = {}
+        codes = {}
+        scales = {}
+        obuf = {}
+        store_of = {}
+        t0 = 0
+        for c, n in enumerate(STORES):
+            for i in range(n):
+                store_of[t0 + i] = (c, i, n, t0)
+            t0 += n
+
+        def transposes(t):
+            bank = psum.tile([P, 512], F32, tag="pt%d" % (t % 4), name="pt_%d" % t)
+            for k in range(4):
+                nc.tensor.transpose(bank[:, k * P:(k + 1) * P], xw[t][:, k * P:(k + 1) * P], ident[:])
+            pt[t] = bank
+
+        def copy_in(t, eng):
+            j, i = divmod(t, GROUP)
+            if i == 0:
+                gr = gpool.tile([P, GROUP * L], BF16, tag="gr", name="gr%d" % j, align_bytes=64)
+                grouped[j] = gr
+            dst = grouped[j][:].bitcast(F32)[:, i * 512:(i + 1) * 512].rearrange("p (g m u) -> p g m u", g=2, u=2)
+            src = pt[t][:].rearrange("p (g u m) -> p g m u", g=2, u=2)
+            if eng == "V":
+                nc.vector.tensor_copy(out=dst, in_=src)
+            else:
+                nc.scalar.copy(out=dst, in_=src)
+
+        def quantise(j):
+            cj = cpool.tile([P, GROUP * 256], U32, name="codes%d" % j, align_bytes=64)
+            sj = cpool.tile([P, GROUP * 256], U8, name="scales%d" % j, align_bytes=64)
+            nc.vector.quantize_mx(out=cj[:].bitcast(FP8X4), scales=sj[:], in_=grouped[j][:])
+            codes[j] = cj
+            scales[j] = sj
+
+        def mx(t, g):
+            j, i = divmod(t, GROUP)
+            if g == 0:
+                acc = psum.tile([P, K], F32, tag="po%d" % (t % 4), name="po_%d" % t)
+                po[t] = acc
+            cols = slice(i * 256 + g * P, i * 256 + (g + 1) * P)
+            nc.tensor.matmul_mx(out=po[t][:], lhsT=codes[j][:, cols].bitcast(FP8X4), lhsT_scale=scales[j][:, cols],
+                                rhs=wcodes[g][:].bitcast(FP8X4), rhs_scale=wscl[g][:],
+                                start=(g == 0), stop=(g == 1))
+
+        def copy_out(t, eng):
+            c, i, n, first = store_of[t]
+            if i == 0:
+                ob = opool.tile([P, n * K], F32, tag="ob%d" % n, name="ob_%d" % c, bufs=(3 if n == 4 else 4))
+                obuf[c] = ob
+            dst = obuf[c][:, i * K:(i + 1) * K]
+            if eng == "V":
+                nc.vector.tensor_copy(out=dst, in_=po[t][:])
+            else:
+                nc.scalar.copy(out=dst, in_=po[t][:])
+            if i == n - 1:
+                nc.sync.dma_start(out=ov[:, first * K:(first + n) * K], in_=obuf[c][:])
+
+        for t in range(4):
+            transposes(t)
+        for t in range(4):
+            copy_in(t, "V")
+            transposes(t + 4)
+        quantise(0)
+        for t in range(4, 8):
+            copy_in(t, "V")
+            transposes(t + 4)
+        quantise(1)
+        copy_in(8, "V")
+        quantise_w(0)
+        for t in range(4):
+            mx(t, 0)
+        transposes(12)
+        for t in range(9, 12):
+            copy_in(t, "V")
+            transposes(t + 4)
+        quantise_w(1)
+        for t in range(4):
+            mx(t, 1)
+        quantise(2)
+        for t in range(12, 15):
+            copy_in(t, "S")
+        copy_in(15, "V")
+        for t in range(4):
+            copy_out(t, "S")
+        for j in range(1, 8):
+            for i in range(4):
+                mx(4 * j + i, 0)
+                mx(4 * j + i, 1)
+            for i in range(4):
+                copy_out(4 * j + i, "V" if (j >= 5 and i % 2 == 1) else "S")
+            if j + 3 < 8:
+                for i in range(4):
+                    transposes(4 * (j + 3) + i)
+            if j + 2 < 8:
+                quantise(j + 2)
+            if j + 3 < 8:
+                for i in range(4):
+                    copy_in(4 * (j + 3) + i, "V")

@@ -10,12 +10,12 @@ U32 = mybir.dt.uint32
 U8 = mybir.dt.uint8
 FP8X4 = mybir.dt.float8_e4m3fn_x4
 ACT = mybir.ActivationFunctionType
+ALU = mybir.AluOpType
 
 P = 128
 ROWS = 4096
 L = 1024
 K = 512
-TILES = ROWS // P
 GROUP = 4
 FLOPS = 2 * ROWS * L * K
 
@@ -37,26 +37,10 @@ def tile_samplinglayer_kernel(tc, x, weight, out):
         psum = ctx.enter_context(tc.psum_pool(name="psum", bufs=1))
         ctx.enter_context(tc.manual_schedule())
 
-        nb_i = const.tile([P, 8], I32, name="nb_i")
-        nc.gpsimd.iota(nb_i[:], pattern=[[-512, 2], [-256, 2], [-1, 2]], base=-1, channel_multiplier=-2)
-        ident = const.tile([P, P], F32, name="ident")
-        make_identity(nc, ident[:])
-
-        zero1 = const.tile([P, 1], F32, name="zero1")
-        nc.vector.memset(zero1[:], 0.0)
-        wz = const.tile([P, K], BF16, name="wz")
-        nc.vector.memset(wz[0:64, :], 0.0)
-        nc.vector.memset(wz[64:96, :], 0.0)
-        nc.vector.memset(wz[96:127, :], 0.0)
-        ones = const.tile([P, P], BF16, name="ones")
-        nc.vector.memset(ones[:], 1.0)
-        nb = const.tile([P, 8], F32, name="nb")
-        nc.vector.tensor_copy(out=nb[:], in_=nb_i[:])
-
-        warm = const.tile([P, 1], F32, name="warm")
-        nc.scalar.activation(out=warm[:], in_=zero1[:], func=ACT.Exp)
-
-        nc.sync.dma_start(out=wz[127:128, :], in_=weight.rearrange("(o n) -> o n", o=1))
+        wr = const.tile([P, K], BF16, name="wr")
+        rhs_w = const.tile([P, K], BF16, name="rhs_w")
+        nc.sync.dma_start(out=wr[126:128, :], in_=weight.partition_broadcast(2))
+        nc.sync.dma_start(out=rhs_w[62:64, :], in_=weight.partition_broadcast(2))
         xw = {}
         t0 = 0
         for c, n in enumerate(LOADS):
@@ -67,25 +51,87 @@ def tile_samplinglayer_kernel(tc, x, weight, out):
                 xw[t0 + i] = words[:, i * (L // 2):(i + 1) * (L // 2)]
             t0 += n
 
-        wbc = psum.tile([P, K], F32, tag="po3", name="wbc")
-        nc.tensor.matmul(out=wbc[:], lhsT=ones[:], rhs=wz[:], start=True, stop=True)
-        sq = const.tile([P, 8 * K], F32, name="sq")
-        for j in range(8):
-            nc.scalar.activation(out=sq[:, j * K:(j + 1) * K], in_=wbc[:], func=ACT.Square,
-                                 bias=nb[:, j:j + 1], scale=1.0)
+        tau_i = const.tile([P, 8], I32, name="tau_i")
+        nc.gpsimd.iota(tau_i[:], pattern=[[512, 2], [256, 2], [1, 2]], base=1, channel_multiplier=2)
+        ident_b = const.tile([P, P], BF16, name="ident_b")
+        make_identity(nc, ident_b[:])
+        ident_f = const.tile([P, P], F32, name="ident_f")
+        make_identity(nc, ident_f[:])
+
+        zero1 = const.tile([P, 1], F32, name="zero1")
+        nc.vector.memset(zero1[:], 0.0)
+        warm = const.tile([P, 1], F32, name="warm")
+        nc.scalar.activation(out=warm[:], in_=zero1[:], func=ACT.Exp)
+
+        ftab = const.tile([P, 8 * P], BF16, name="ftab")
+        nc.vector.memset(ftab[:], 0.0)
+        f3 = ftab[:].rearrange("p (j k) -> p j k", k=P)
+        tau = const.tile([P, 8], F32, name="tau")
+        nc.vector.tensor_copy(out=tau[:], in_=tau_i[:])
+        tau2 = const.tile([P, 8], F32, name="tau2")
+        nc.vector.tensor_tensor(out=tau2[:], in0=tau[:], in1=tau[:], op=ALU.mult)
+        nc.vector.tensor_copy(out=f3[:, :, 0], in_=tau2[:])
+        rest = const.tile([P, 8], F32, name="rest")
+        nc.vector.tensor_tensor(out=rest[:], in0=tau2[:], in1=f3[:, :, 0], op=ALU.subtract)
+        nc.vector.tensor_copy(out=f3[:, :, 1], in_=rest[:])
+        nc.vector.tensor_tensor(out=f3[:, :, 2], in0=rest[:], in1=f3[:, :, 1], op=ALU.subtract)
+        nc.vector.tensor_scalar(out=f3[:, :, 62], in0=tau[:], scalar1=-2.0, scalar2=None, op0=ALU.mult)
+        nc.vector.scalar_tensor_tensor(out=f3[:, :, 63], in0=tau[:], scalar=-2.0, in1=f3[:, :, 62],
+                                       op0=ALU.mult, op1=ALU.subtract)
+        nc.vector.memset(f3[:, :, 126:128], 1.0)
+
+        tabps = []
+        tab = []
+        for g in range(2):
+            tp = psum.tile([P, 4 * P], BF16, tag="po%d" % g, name="tabps%d" % g)
+            for t in range(4):
+                j = 4 * g + t
+                nc.tensor.transpose(tp[:, t * P:(t + 1) * P], ftab[:, j * P:(j + 1) * P], ident_b[:])
+            tabps.append(tp)
+            tb = const.tile([P, 4 * P], BF16, name="tab%d" % g)
+            tab.append(tb)
+
+        nc.vector.memset(wr[96:126, :], 0.0)
+        nc.vector.memset(rhs_w[0:32, :], 1.0)
+        nc.vector.memset(rhs_w[32:62, :], 0.0)
+        nc.vector.memset(rhs_w[64:96, :], 0.0)
+        sgn = const.tile([P, 1], F32, name="sgn")
+        nc.vector.tensor_tensor(out=sgn[:], in0=ident_f[:, 126:127], in1=ident_f[:, 127:128], op=ALU.subtract)
+
+        hi = const.tile([P, K], BF16, name="hi")
+        nc.vector.tensor_tensor(out=hi[96:128, :], in0=wr[96:128, :], in1=wr[96:128, :], op=ALU.mult)
+        ysq = const.tile([P, K], F32, name="ysq")
+        nc.scalar.activation(out=ysq[96:128, :], in_=wr[96:128, :], func=ACT.Square,
+                             scale=ident_f[96:128, 127:128])
+        nc.vector.tensor_copy(out=tab[0][:], in_=tabps[0][:])
+        nc.scalar.copy(out=tab[1][:], in_=tabps[1][:])
+        nc.vector.scalar_tensor_tensor(out=rhs_w[96:128, :], in0=hi[96:128, :], scalar=sgn[96:128, 0:1],
+                                       in1=ysq[96:128, :], op0=ALU.mult, op1=ALU.add)
+
         wg = []
         wcodes = []
         wscl = []
         for g in range(2):
             wg_g = const.tile([P, 4 * K], BF16, name="wg%d" % g, align_bytes=64)
-            nc.scalar.activation(out=wg_g[:].rearrange("p (n t) -> p n t", t=4),
-                                 in_=sq[:, g * 4 * K:(g + 1) * 4 * K].rearrange("p (t n) -> p n t", t=4),
-                                 func=ACT.Exp, scale=-0.01)
-            wg.append(wg_g)
             wc_g = const.tile([P, K], U32, name="wcodes%d" % g, align_bytes=64)
             ws_g = const.tile([P, K], U8, name="wscl%d" % g, align_bytes=64)
+            wg.append(wg_g)
             wcodes.append(wc_g)
             wscl.append(ws_g)
+        wbank = {}
+
+        def distances(b):
+            g, nb = divmod(b, 4)
+            bank = psum.tile([P, 512], F32, tag="po%d" % ((b + 2) % 4), name="wd%d" % b)
+            bv = bank[:].rearrange("p (n t) -> p n t", t=4)
+            for t in range(4):
+                nc.tensor.matmul(out=bv[:, :, t], lhsT=tab[g][:, t * P:(t + 1) * P],
+                                 rhs=rhs_w[:, nb * P:(nb + 1) * P], start=True, stop=True)
+            wbank[b] = bank
+
+        def gauss(b):
+            g, nb = divmod(b, 4)
+            nc.scalar.activation(out=wg[g][:, nb * 512:(nb + 1) * 512], in_=wbank[b][:], func=ACT.Exp, scale=-0.01)
 
         def quantise_w(g):
             nc.vector.quantize_mx(out=wcodes[g][:].bitcast(FP8X4), scales=wscl[g][:], in_=wg[g][:])
@@ -106,7 +152,7 @@ def tile_samplinglayer_kernel(tc, x, weight, out):
         def transposes(t):
             bank = psum.tile([P, 512], F32, tag="pt%d" % (t % 4), name="pt_%d" % t)
             for k in range(4):
-                nc.tensor.transpose(bank[:, k * P:(k + 1) * P], xw[t][:, k * P:(k + 1) * P], ident[:])
+                nc.tensor.transpose(bank[:, k * P:(k + 1) * P], xw[t][:, k * P:(k + 1) * P], ident_f[:])
             pt[t] = bank
 
         def copy_in(t, eng):
@@ -151,44 +197,48 @@ def tile_samplinglayer_kernel(tc, x, weight, out):
             if i == n - 1:
                 nc.sync.dma_start(out=ov[:, first * K:(first + n) * K], in_=obuf[c][:])
 
-        for t in range(4):
-            transposes(t)
+        transposes(0)
+        transposes(1)
+        for b in range(4):
+            distances(b)
+        transposes(2)
+        transposes(3)
+        for b in range(8):
+            gauss(b)
+            if b + 4 < 8:
+                distances(b + 4)
         for t in range(4):
             copy_in(t, "V")
             transposes(t + 4)
-        quantise(0)
-        for t in range(4, 8):
-            copy_in(t, "V")
-            transposes(t + 4)
-        quantise(1)
-        copy_in(8, "V")
         quantise_w(0)
-        for t in range(4):
-            mx(t, 0)
-        transposes(12)
-        for t in range(9, 12):
-            copy_in(t, "V")
-            transposes(t + 4)
+        quantise(0)
+        copy_in(4, "V")
+        transposes(8)
         quantise_w(1)
-        for t in range(4):
-            mx(t, 1)
+        copy_in(5, "S")
+        transposes(9)
+        copy_in(6, "S")
+        transposes(10)
+        copy_in(7, "V")
+        transposes(11)
+        copy_in(8, "S")
+        copy_in(9, "S")
+        copy_in(10, "V")
+        copy_in(11, "S")
+        quantise(1)
         quantise(2)
-        for t in range(12, 15):
-            copy_in(t, "S")
-        copy_in(15, "V")
-        for t in range(4):
-            copy_out(t, "S")
-        for j in range(1, 8):
+        for j in range(8):
             for i in range(4):
                 mx(4 * j + i, 0)
                 mx(4 * j + i, 1)
-            for i in range(4):
-                copy_out(4 * j + i, "V" if (j >= 5 and i % 2 == 1) else "S")
             if j + 3 < 8:
                 for i in range(4):
                     transposes(4 * (j + 3) + i)
-            if j + 2 < 8:
+            for i in range(4):
+                on_vector = (i % 2 == 0) if j >= 5 else (i == 0)
+                copy_out(4 * j + i, "V" if on_vector else "S")
+            if j >= 1 and j + 2 < 8:
                 quantise(j + 2)
             if j + 3 < 8:
                 for i in range(4):
-                    copy_in(4 * (j + 3) + i, "V")
+                    copy_in(4 * (j + 3) + i, "V" if i % 2 == 0 else "S")

@@ -66,19 +66,23 @@ def tile_samplinglayer_kernel(tc, x, weight, out):
         ftab = const.tile([P, 8 * P], BF16, name="ftab")
         nc.vector.memset(ftab[:], 0.0)
         f3 = ftab[:].rearrange("p (j k) -> p j k", k=P)
+        nc.vector.memset(f3[:, :, 126:128], 1.0)
+        nc.vector.memset(wr[96:126, :], 0.0)
+        nc.vector.memset(rhs_w[0:32, :], 1.0)
+        nc.vector.memset(rhs_w[32:62, :], 0.0)
+        nc.vector.memset(rhs_w[64:96, :], 0.0)
         tau = const.tile([P, 8], F32, name="tau")
         nc.vector.tensor_copy(out=tau[:], in_=tau_i[:])
         tau2 = const.tile([P, 8], F32, name="tau2")
         nc.vector.tensor_tensor(out=tau2[:], in0=tau[:], in1=tau[:], op=ALU.mult)
+        nc.vector.tensor_scalar(out=f3[:, :, 62], in0=tau[:], scalar1=-2.0, scalar2=None, op0=ALU.mult)
         nc.vector.tensor_copy(out=f3[:, :, 0], in_=tau2[:])
+        nc.vector.scalar_tensor_tensor(out=f3[:, :, 63], in0=tau[:], scalar=-2.0, in1=f3[:, :, 62],
+                                       op0=ALU.mult, op1=ALU.subtract)
         rest = const.tile([P, 8], F32, name="rest")
         nc.vector.tensor_tensor(out=rest[:], in0=tau2[:], in1=f3[:, :, 0], op=ALU.subtract)
         nc.vector.tensor_copy(out=f3[:, :, 1], in_=rest[:])
         nc.vector.tensor_tensor(out=f3[:, :, 2], in0=rest[:], in1=f3[:, :, 1], op=ALU.subtract)
-        nc.vector.tensor_scalar(out=f3[:, :, 62], in0=tau[:], scalar1=-2.0, scalar2=None, op0=ALU.mult)
-        nc.vector.scalar_tensor_tensor(out=f3[:, :, 63], in0=tau[:], scalar=-2.0, in1=f3[:, :, 62],
-                                       op0=ALU.mult, op1=ALU.subtract)
-        nc.vector.memset(f3[:, :, 126:128], 1.0)
 
         tabps = []
         tab = []
@@ -91,22 +95,17 @@ def tile_samplinglayer_kernel(tc, x, weight, out):
             tb = const.tile([P, 4 * P], BF16, name="tab%d" % g)
             tab.append(tb)
 
-        nc.vector.memset(wr[96:126, :], 0.0)
-        nc.vector.memset(rhs_w[0:32, :], 1.0)
-        nc.vector.memset(rhs_w[32:62, :], 0.0)
-        nc.vector.memset(rhs_w[64:96, :], 0.0)
         sgn = const.tile([P, 1], F32, name="sgn")
         nc.vector.tensor_tensor(out=sgn[:], in0=ident_f[:, 126:127], in1=ident_f[:, 127:128], op=ALU.subtract)
-
         hi = const.tile([P, K], BF16, name="hi")
         nc.vector.tensor_tensor(out=hi[96:128, :], in0=wr[96:128, :], in1=wr[96:128, :], op=ALU.mult)
         ysq = const.tile([P, K], F32, name="ysq")
         nc.scalar.activation(out=ysq[96:128, :], in_=wr[96:128, :], func=ACT.Square,
                              scale=ident_f[96:128, 127:128])
-        nc.vector.tensor_copy(out=tab[0][:], in_=tabps[0][:])
-        nc.scalar.copy(out=tab[1][:], in_=tabps[1][:])
         nc.vector.scalar_tensor_tensor(out=rhs_w[96:128, :], in0=hi[96:128, :], scalar=sgn[96:128, 0:1],
                                        in1=ysq[96:128, :], op0=ALU.mult, op1=ALU.add)
+        nc.vector.tensor_copy(out=tab[0][:], in_=tabps[0][:])
+        nc.vector.tensor_copy(out=tab[1][:], in_=tabps[1][:])
 
         wg = []
         wcodes = []
@@ -197,35 +196,29 @@ def tile_samplinglayer_kernel(tc, x, weight, out):
             if i == n - 1:
                 nc.sync.dma_start(out=ov[:, first * K:(first + n) * K], in_=obuf[c][:])
 
-        transposes(0)
-        transposes(1)
+        for t in range(4):
+            transposes(t)
+        for t in range(4):
+            copy_in(t, "S")
         for b in range(4):
             distances(b)
-        transposes(2)
-        transposes(3)
-        for b in range(8):
+        for b in range(4):
             gauss(b)
-            if b + 4 < 8:
-                distances(b + 4)
-        for t in range(4):
-            copy_in(t, "V")
-            transposes(t + 4)
-        quantise_w(0)
+            distances(b + 4)
+            transposes(b + 4)
+        for b in range(4, 8):
+            gauss(b)
         quantise(0)
         copy_in(4, "V")
         transposes(8)
+        quantise_w(0)
+        for t in range(5, 8):
+            copy_in(t, "V")
+            transposes(t + 4)
         quantise_w(1)
-        copy_in(5, "S")
-        transposes(9)
-        copy_in(6, "S")
-        transposes(10)
-        copy_in(7, "V")
-        transposes(11)
-        copy_in(8, "S")
-        copy_in(9, "S")
-        copy_in(10, "V")
-        copy_in(11, "S")
         quantise(1)
+        for t in range(8, 12):
+            copy_in(t, "S")
         quantise(2)
         for j in range(8):
             for i in range(4):

@@ -39,85 +39,55 @@ def tile_samplinglayer_kernel(tc, x, weight, out):
 
         wr = const.tile([P, K], BF16, name="wr")
         rhs_w = const.tile([P, K], BF16, name="rhs_w")
-        nc.sync.dma_start(out=wr[126:128, :], in_=weight.partition_broadcast(2))
-        nc.sync.dma_start(out=rhs_w[62:64, :], in_=weight.partition_broadcast(2))
-        xw = {}
-        t0 = 0
-        for c, n in enumerate(LOADS):
-            xt = xpool.tile([P, n * L], BF16, name="x%d" % c)
-            nc.sync.dma_start(out=xt[:], in_=xv[:, t0 * L:(t0 + n) * L])
-            words = xt[:].bitcast(F32)
-            for i in range(n):
-                xw[t0 + i] = words[:, i * (L // 2):(i + 1) * (L // 2)]
-            t0 += n
-
         tau_i = const.tile([P, 8], I32, name="tau_i")
-        nc.gpsimd.iota(tau_i[:], pattern=[[512, 2], [256, 2], [1, 2]], base=1, channel_multiplier=2)
-        ident_b = const.tile([P, P], BF16, name="ident_b")
-        make_identity(nc, ident_b[:])
         ident_f = const.tile([P, P], F32, name="ident_f")
-        make_identity(nc, ident_f[:])
-
+        ident_b = const.tile([P, P], BF16, name="ident_b")
         zero1 = const.tile([P, 1], F32, name="zero1")
-        nc.vector.memset(zero1[:], 0.0)
         warm = const.tile([P, 1], F32, name="warm")
-        nc.scalar.activation(out=warm[:], in_=zero1[:], func=ACT.Exp)
-
         ftab = const.tile([P, 8 * P], BF16, name="ftab")
-        nc.vector.memset(ftab[:], 0.0)
         f3 = ftab[:].rearrange("p (j k) -> p j k", k=P)
-        nc.vector.memset(f3[:, :, 126:128], 1.0)
-        nc.vector.memset(wr[96:126, :], 0.0)
-        nc.vector.memset(rhs_w[0:32, :], 1.0)
-        nc.vector.memset(rhs_w[32:62, :], 0.0)
-        nc.vector.memset(rhs_w[64:96, :], 0.0)
         tau = const.tile([P, 8], F32, name="tau")
-        nc.vector.tensor_copy(out=tau[:], in_=tau_i[:])
         tau2 = const.tile([P, 8], F32, name="tau2")
-        nc.vector.tensor_tensor(out=tau2[:], in0=tau[:], in1=tau[:], op=ALU.mult)
-        nc.vector.tensor_scalar(out=f3[:, :, 62], in0=tau[:], scalar1=-2.0, scalar2=None, op0=ALU.mult)
-        nc.vector.tensor_copy(out=f3[:, :, 0], in_=tau2[:])
-        nc.vector.scalar_tensor_tensor(out=f3[:, :, 63], in0=tau[:], scalar=-2.0, in1=f3[:, :, 62],
-                                       op0=ALU.mult, op1=ALU.subtract)
         rest = const.tile([P, 8], F32, name="rest")
-        nc.vector.tensor_tensor(out=rest[:], in0=tau2[:], in1=f3[:, :, 0], op=ALU.subtract)
-        nc.vector.tensor_copy(out=f3[:, :, 1], in_=rest[:])
-        nc.vector.tensor_tensor(out=f3[:, :, 2], in0=rest[:], in1=f3[:, :, 1], op=ALU.subtract)
-
-        tabps = []
-        tab = []
-        for g in range(2):
-            tp = psum.tile([P, 4 * P], BF16, tag="po%d" % g, name="tabps%d" % g)
-            for t in range(4):
-                j = 4 * g + t
-                nc.tensor.transpose(tp[:, t * P:(t + 1) * P], ftab[:, j * P:(j + 1) * P], ident_b[:])
-            tabps.append(tp)
-            tb = const.tile([P, 4 * P], BF16, name="tab%d" % g)
-            tab.append(tb)
-
         sgn = const.tile([P, 1], F32, name="sgn")
-        nc.vector.tensor_tensor(out=sgn[:], in0=ident_f[:, 126:127], in1=ident_f[:, 127:128], op=ALU.subtract)
         hi = const.tile([P, K], BF16, name="hi")
-        nc.vector.tensor_tensor(out=hi[96:128, :], in0=wr[96:128, :], in1=wr[96:128, :], op=ALU.mult)
         ysq = const.tile([P, K], F32, name="ysq")
-        nc.scalar.activation(out=ysq[96:128, :], in_=wr[96:128, :], func=ACT.Square,
-                             scale=ident_f[96:128, 127:128])
-        nc.vector.scalar_tensor_tensor(out=rhs_w[96:128, :], in0=hi[96:128, :], scalar=sgn[96:128, 0:1],
-                                       in1=ysq[96:128, :], op0=ALU.mult, op1=ALU.add)
-        nc.vector.tensor_copy(out=tab[0][:], in_=tabps[0][:])
-        nc.vector.tensor_copy(out=tab[1][:], in_=tabps[1][:])
-
+        tab = []
         wg = []
         wcodes = []
         wscl = []
         for g in range(2):
+            tb = const.tile([P, 4 * P], BF16, name="tab%d" % g)
             wg_g = const.tile([P, 4 * K], BF16, name="wg%d" % g, align_bytes=64)
             wc_g = const.tile([P, K], U32, name="wcodes%d" % g, align_bytes=64)
             ws_g = const.tile([P, K], U8, name="wscl%d" % g, align_bytes=64)
+            tab.append(tb)
             wg.append(wg_g)
             wcodes.append(wc_g)
             wscl.append(ws_g)
+
+        xw = {}
+        tabps = {}
         wbank = {}
+        pt = {}
+        po = {}
+        grouped = {}
+        codes = {}
+        scales = {}
+        obuf = {}
+        store_of = {}
+        t0 = 0
+        for c, n in enumerate(STORES):
+            for i in range(n):
+                store_of[t0 + i] = (c, i, n, t0)
+            t0 += n
+
+        def table_transposes(g):
+            tp = psum.tile([P, 4 * P], BF16, tag="po%d" % g, name="tabps%d" % g)
+            for t in range(4):
+                j = 4 * g + t
+                nc.tensor.transpose(tp[:, t * P:(t + 1) * P], ftab[:, j * P:(j + 1) * P], ident_b[:])
+            tabps[g] = tp
 
         def distances(b):
             g, nb = divmod(b, 4)
@@ -134,19 +104,6 @@ def tile_samplinglayer_kernel(tc, x, weight, out):
 
         def quantise_w(g):
             nc.vector.quantize_mx(out=wcodes[g][:].bitcast(FP8X4), scales=wscl[g][:], in_=wg[g][:])
-
-        pt = {}
-        po = {}
-        grouped = {}
-        codes = {}
-        scales = {}
-        obuf = {}
-        store_of = {}
-        t0 = 0
-        for c, n in enumerate(STORES):
-            for i in range(n):
-                store_of[t0 + i] = (c, i, n, t0)
-            t0 += n
 
         def transposes(t):
             bank = psum.tile([P, 512], F32, tag="pt%d" % (t % 4), name="pt_%d" % t)
@@ -196,10 +153,59 @@ def tile_samplinglayer_kernel(tc, x, weight, out):
             if i == n - 1:
                 nc.sync.dma_start(out=ov[:, first * K:(first + n) * K], in_=obuf[c][:])
 
-        for t in range(4):
-            transposes(t)
-        for t in range(4):
-            copy_in(t, "S")
+        nc.sync.dma_start(out=wr[126:128, :], in_=weight.partition_broadcast(2))
+        nc.sync.dma_start(out=rhs_w[62:64, :], in_=weight.partition_broadcast(2))
+        t0 = 0
+        for c, n in enumerate(LOADS):
+            xt = xpool.tile([P, n * L], BF16, name="x%d" % c)
+            nc.sync.dma_start(out=xt[:], in_=xv[:, t0 * L:(t0 + n) * L])
+            words = xt[:].bitcast(F32)
+            for i in range(n):
+                xw[t0 + i] = words[:, i * (L // 2):(i + 1) * (L // 2)]
+            t0 += n
+
+        nc.gpsimd.iota(tau_i[:], pattern=[[512, 2], [256, 2], [1, 2]], base=1, channel_multiplier=2)
+        nc.gpsimd.memset(wr[96:126, :], 0.0)
+        make_identity(nc, ident_f[:])
+        make_identity(nc, ident_b[:])
+        nc.gpsimd.memset(rhs_w[0:32, :], 1.0)
+        nc.gpsimd.memset(rhs_w[32:62, :], 0.0)
+        nc.gpsimd.memset(rhs_w[64:96, :], 0.0)
+
+        nc.vector.memset(zero1[:], 0.0)
+        nc.scalar.activation(out=warm[:], in_=zero1[:], func=ACT.Exp)
+        nc.vector.memset(ftab[:], 0.0)
+        nc.vector.memset(f3[:, :, 126:128], 1.0)
+        nc.vector.tensor_copy(out=tau[:], in_=tau_i[:])
+        nc.vector.tensor_tensor(out=tau2[:], in0=tau[:], in1=tau[:], op=ALU.mult)
+        nc.vector.tensor_scalar(out=f3[:, :, 62], in0=tau[:], scalar1=-2.0, scalar2=None, op0=ALU.mult)
+        nc.vector.tensor_copy(out=f3[:, :, 0], in_=tau2[:])
+        nc.vector.scalar_tensor_tensor(out=f3[:, :, 63], in0=tau[:], scalar=-2.0, in1=f3[:, :, 62],
+                                       op0=ALU.mult, op1=ALU.subtract)
+        nc.vector.tensor_tensor(out=rest[:], in0=tau2[:], in1=f3[:, :, 0], op=ALU.subtract)
+        nc.vector.tensor_copy(out=f3[:, :, 1], in_=rest[:])
+        nc.vector.tensor_tensor(out=f3[:, :, 2], in0=rest[:], in1=f3[:, :, 1], op=ALU.subtract)
+
+        transposes(0)
+        transposes(1)
+        table_transposes(0)
+        table_transposes(1)
+        transposes(2)
+        transposes(3)
+
+        nc.vector.tensor_tensor(out=sgn[:], in0=ident_f[:, 126:127], in1=ident_f[:, 127:128], op=ALU.subtract)
+        nc.vector.tensor_tensor(out=hi[96:128, :], in0=wr[96:128, :], in1=wr[96:128, :], op=ALU.mult)
+        nc.scalar.activation(out=ysq[96:128, :], in_=wr[96:128, :], func=ACT.Square,
+                             scale=ident_f[96:128, 127:128])
+        nc.vector.scalar_tensor_tensor(out=rhs_w[96:128, :], in0=hi[96:128, :], scalar=sgn[96:128, 0:1],
+                                       in1=ysq[96:128, :], op0=ALU.mult, op1=ALU.add)
+        copy_in(0, "S")
+        copy_in(1, "S")
+        nc.scalar.copy(out=tab[0][:], in_=tabps[0][:])
+        nc.scalar.copy(out=tab[1][:], in_=tabps[1][:])
+        copy_in(2, "S")
+        copy_in(3, "S")
+
         for b in range(4):
             distances(b)
         for b in range(4):

@@ -43,6 +43,7 @@ def tile_samplinglayer_kernel(tc, x, weight, out):
         ident_f = const.tile([P, P], F32, name="ident_f")
         ident_b = const.tile([P, P], BF16, name="ident_b")
         zero1 = const.tile([P, 1], F32, name="zero1")
+        idle = const.tile([P, K], BF16, name="idle")
         warm = const.tile([P, 1], F32, name="warm")
         ftab = const.tile([P, 8 * P], BF16, name="ftab")
         f3 = ftab[:].rearrange("p (j k) -> p j k", k=P)
@@ -88,6 +89,11 @@ def tile_samplinglayer_kernel(tc, x, weight, out):
                 j = 4 * g + t
                 nc.tensor.transpose(tp[:, t * P:(t + 1) * P], ftab[:, j * P:(j + 1) * P], ident_b[:])
             tabps[g] = tp
+
+        def keep_clock_up(n):
+            spare = psum.tile([P, K], F32, tag="pt3", name="spare")
+            for i in range(n):
+                nc.tensor.matmul(out=spare[:], lhsT=idle[:, 0:P], rhs=idle[:], start=True, stop=True)
 
         def distances(b):
             g, nb = divmod(b, 4)
@@ -172,6 +178,7 @@ def tile_samplinglayer_kernel(tc, x, weight, out):
         nc.gpsimd.memset(rhs_w[32:62, :], 0.0)
         nc.gpsimd.memset(rhs_w[64:96, :], 0.0)
 
+        nc.vector.memset(idle[:], 0.0)
         nc.vector.memset(zero1[:], 0.0)
         nc.scalar.activation(out=warm[:], in_=zero1[:], func=ACT.Exp)
         nc.vector.memset(ftab[:], 0.0)
@@ -186,10 +193,13 @@ def tile_samplinglayer_kernel(tc, x, weight, out):
         nc.vector.tensor_copy(out=f3[:, :, 1], in_=rest[:])
         nc.vector.tensor_tensor(out=f3[:, :, 2], in0=rest[:], in1=f3[:, :, 1], op=ALU.subtract)
 
+        keep_clock_up(5)
         transposes(0)
         transposes(1)
+        keep_clock_up(1)
         table_transposes(0)
         table_transposes(1)
+        keep_clock_up(1)
         transposes(2)
         transposes(3)
 

@@ -20,7 +20,9 @@ GROUP = 4
 FLOPS = 2 * ROWS * L * K
 
 LOADS = [1, 1, 2, 4, 4, 4, 4, 4, 4, 4]
-STORES = [4, 4, 4, 4, 4, 2, 2, 2, 2, 1, 1, 1, 1]
+STORES = [4, 4, 4, 4, 4, 2, 2, 2, 2, 1, 1, 1]
+TILES = ROWS // P
+HALVED = 2
 
 
 def tile_samplinglayer_kernel(tc, x, weight, out):
@@ -159,6 +161,34 @@ def tile_samplinglayer_kernel(tc, x, weight, out):
             if i == n - 1:
                 nc.sync.dma_start(out=ov[:, first * K:(first + n) * K], in_=obuf[c][:])
 
+        def mx_half(t, h):
+            j, i = divmod(t, GROUP)
+            acc = psum.tile([P, K], F32, tag=("po%d" if h == 0 else "pt%d") % (t % 4), name="po_%d_%d" % (t, h))
+            po[t, h] = acc
+            for g in range(2):
+                cols = slice(i * 256 + g * P, i * 256 + (g + 1) * P)
+                half = slice(h * 256, (h + 1) * 256)
+                nc.tensor.matmul_mx(out=acc[:, 0:256], lhsT=codes[j][:, cols].bitcast(FP8X4),
+                                    lhsT_scale=scales[j][:, cols],
+                                    rhs=wcodes[g][:, half].bitcast(FP8X4), rhs_scale=wscl[g][:, half],
+                                    start=(g == 0), stop=(g == 1))
+
+        def copy_half(t, h):
+            last = t == TILES - 1
+            if h == 0 and not last:
+                obuf[t] = opool.tile([P, K], F32, tag="ob1", name="ob_t%d" % t, bufs=4)
+            if last:
+                obuf[t] = opool.tile([P, 256], F32, tag="obh", name="ob_t%d_%d" % (t, h), bufs=2)
+            dst = obuf[t][:] if last else obuf[t][:, h * 256:(h + 1) * 256]
+            if h == 0:
+                nc.vector.tensor_copy(out=dst, in_=po[t, h][:, 0:256])
+            else:
+                nc.scalar.copy(out=dst, in_=po[t, h][:, 0:256])
+            if last:
+                nc.sync.dma_start(out=ov[:, t * K + h * 256:t * K + (h + 1) * 256], in_=obuf[t][:])
+            elif h == 1:
+                nc.sync.dma_start(out=ov[:, t * K:(t + 1) * K], in_=obuf[t][:])
+
         nc.sync.dma_start(out=wr[126:128, :], in_=weight.partition_broadcast(2))
         nc.sync.dma_start(out=rhs_w[62:64, :], in_=weight.partition_broadcast(2))
         t0 = 0
@@ -238,14 +268,22 @@ def tile_samplinglayer_kernel(tc, x, weight, out):
         quantise(2)
         for j in range(8):
             for i in range(4):
-                mx(4 * j + i, 0)
-                mx(4 * j + i, 1)
+                if 4 * j + i < TILES - HALVED:
+                    mx(4 * j + i, 0)
+                    mx(4 * j + i, 1)
+                else:
+                    mx_half(4 * j + i, 0)
+                    mx_half(4 * j + i, 1)
             if j + 3 < 8:
                 for i in range(4):
                     transposes(4 * (j + 3) + i)
             for i in range(4):
                 on_vector = (i % 2 == 0) if j >= 5 else (i == 0)
-                copy_out(4 * j + i, "V" if on_vector else "S")
+                if 4 * j + i < TILES - HALVED:
+                    copy_out(4 * j + i, "V" if on_vector else "S")
+                else:
+                    copy_half(4 * j + i, 0)
+                    copy_half(4 * j + i, 1)
             if j >= 1 and j + 2 < 8:
                 quantise(j + 2)
             if j + 3 < 8:

@@ -19,7 +19,7 @@ K = 512
 GROUP = 4
 FLOPS = 2 * ROWS * L * K
 
-LOADS = [1, 1, 2, 4, 4, 4, 4, 4, 4, 4]
+LOADS = [1, 1, 1, 1, 2, 2, 4, 4, 4, 4, 4, 4]
 STORES = [4, 4, 4, 4, 4, 2, 2, 2, 2, 1, 1, 1]
 TILES = ROWS // P
 HALVED = 2
@@ -201,17 +201,17 @@ def tile_samplinglayer_kernel(tc, x, weight, out):
             t0 += n
 
         nc.gpsimd.iota(tau_i[:], pattern=[[512, 2], [256, 2], [1, 2]], base=1, channel_multiplier=2)
-        nc.gpsimd.memset(wr[96:126, :], 0.0)
+        nc.gpsimd.memset(wr[96:126, :].bitcast(U32), 0)
         make_identity(nc, ident_f[:])
         make_identity(nc, ident_b[:])
         nc.gpsimd.memset(rhs_w[0:32, :], 1.0)
-        nc.gpsimd.memset(rhs_w[32:62, :], 0.0)
-        nc.gpsimd.memset(rhs_w[64:96, :], 0.0)
+        nc.gpsimd.memset(rhs_w[32:62, :].bitcast(U32), 0)
+        nc.gpsimd.memset(rhs_w[64:96, :].bitcast(U32), 0)
 
-        nc.vector.memset(idle[:], 0.0)
         nc.vector.memset(zero1[:], 0.0)
+        nc.vector.memset(idle[:].bitcast(U32), 0)
         nc.scalar.activation(out=warm[:], in_=zero1[:], func=ACT.Exp)
-        nc.vector.memset(ftab[:], 0.0)
+        nc.vector.memset(ftab[:].bitcast(U32), 0)
         nc.vector.memset(f3[:, :, 126:128], 1.0)
         nc.vector.tensor_copy(out=tau[:], in_=tau_i[:])
         nc.vector.tensor_tensor(out=tau2[:], in0=tau[:], in1=tau[:], op=ALU.mult)
@@ -220,47 +220,48 @@ def tile_samplinglayer_kernel(tc, x, weight, out):
         nc.vector.scalar_tensor_tensor(out=f3[:, :, 63], in0=tau[:], scalar=-2.0, in1=f3[:, :, 62],
                                        op0=ALU.mult, op1=ALU.subtract)
         nc.vector.tensor_tensor(out=rest[:], in0=tau2[:], in1=f3[:, :, 0], op=ALU.subtract)
+        nc.vector.tensor_tensor(out=sgn[:], in0=ident_f[:, 126:127], in1=ident_f[:, 127:128], op=ALU.subtract)
         nc.vector.tensor_copy(out=f3[:, :, 1], in_=rest[:])
+        nc.vector.tensor_tensor(out=hi[96:128, :], in0=wr[96:128, :], in1=wr[96:128, :], op=ALU.mult)
         nc.vector.tensor_tensor(out=f3[:, :, 2], in0=rest[:], in1=f3[:, :, 1], op=ALU.subtract)
 
-        keep_clock_up(5)
+        keep_clock_up(4)
         transposes(0)
         transposes(1)
-        keep_clock_up(1)
         table_transposes(0)
         table_transposes(1)
-        keep_clock_up(1)
         transposes(2)
         transposes(3)
 
-        nc.vector.tensor_tensor(out=sgn[:], in0=ident_f[:, 126:127], in1=ident_f[:, 127:128], op=ALU.subtract)
-        nc.vector.tensor_tensor(out=hi[96:128, :], in0=wr[96:128, :], in1=wr[96:128, :], op=ALU.mult)
         nc.scalar.activation(out=ysq[96:128, :], in_=wr[96:128, :], func=ACT.Square,
                              scale=ident_f[96:128, 127:128])
         nc.vector.scalar_tensor_tensor(out=rhs_w[96:128, :], in0=hi[96:128, :], scalar=sgn[96:128, 0:1],
                                        in1=ysq[96:128, :], op0=ALU.mult, op1=ALU.add)
         copy_in(0, "S")
-        copy_in(1, "S")
         nc.scalar.copy(out=tab[0][:], in_=tabps[0][:])
         nc.scalar.copy(out=tab[1][:], in_=tabps[1][:])
-        copy_in(2, "S")
-        copy_in(3, "S")
+        copy_in(1, "V")
+        copy_in(2, "V")
+        copy_in(3, "V")
+        quantise(0)
 
         for b in range(4):
             distances(b)
         for b in range(4):
+            transposes(b + 4)
             gauss(b)
             distances(b + 4)
-            transposes(b + 4)
         for b in range(4, 8):
             gauss(b)
-        quantise(0)
         copy_in(4, "V")
         transposes(8)
+        copy_in(5, "V")
+        transposes(9)
         quantise_w(0)
-        for t in range(5, 8):
-            copy_in(t, "V")
-            transposes(t + 4)
+        copy_in(6, "V")
+        transposes(10)
+        copy_in(7, "V")
+        transposes(11)
         quantise_w(1)
         quantise(1)
         for t in range(8, 12):

@@ -100,15 +100,16 @@ def tile_samplinglayer_kernel(tc, x, weight, out):
         def distances(b):
             g, nb = divmod(b, 4)
             bank = psum.tile([P, 512], F32, tag="po%d" % ((b + 2) % 4), name="wd%d" % b)
-            bv = bank[:].rearrange("p (n t) -> p n t", t=4)
             for t in range(4):
-                nc.tensor.matmul(out=bv[:, :, t], lhsT=tab[g][:, t * P:(t + 1) * P],
+                nc.tensor.matmul(out=bank[:, t * P:(t + 1) * P], lhsT=tab[g][:, t * P:(t + 1) * P],
                                  rhs=rhs_w[:, nb * P:(nb + 1) * P], start=True, stop=True)
             wbank[b] = bank
 
         def gauss(b):
             g, nb = divmod(b, 4)
-            nc.scalar.activation(out=wg[g][:, nb * 512:(nb + 1) * 512], in_=wbank[b][:], func=ACT.Exp, scale=-0.01)
+            grouped_w = wg[g][:, nb * 512:(nb + 1) * 512].rearrange("p (n t) -> p n t", t=4)
+            nc.scalar.activation(out=grouped_w, in_=wbank[b][:].rearrange("p (t n) -> p n t", t=4), func=ACT.Exp,
+                                 scale=-0.01)
 
         def quantise_w(g):
             nc.vector.quantize_mx(out=wcodes[g][:].bitcast(FP8X4), scales=wscl[g][:], in_=wg[g][:])

@@ -5,7 +5,6 @@ from concourse.masks import make_identity
 
 F32 = mybir.dt.float32
 BF16 = mybir.dt.bfloat16
-I32 = mybir.dt.int32
 U32 = mybir.dt.uint32
 U8 = mybir.dt.uint8
 FP8X4 = mybir.dt.float8_e4m3fn_x4
@@ -41,7 +40,6 @@ def tile_samplinglayer_kernel(tc, x, weight, out):
 
         wr = const.tile([P, K], BF16, name="wr")
         rhs_w = const.tile([P, K], BF16, name="rhs_w")
-        tau_i = const.tile([P, 8], I32, name="tau_i")
         ident_f = const.tile([P, P], F32, name="ident_f")
         ident_b = const.tile([P, P], BF16, name="ident_b")
         zero1 = const.tile([P, 1], F32, name="zero1")
@@ -49,9 +47,10 @@ def tile_samplinglayer_kernel(tc, x, weight, out):
         warm = const.tile([P, 1], F32, name="warm")
         ftab = const.tile([P, 8 * P], BF16, name="ftab")
         f3 = ftab[:].rearrange("p (j k) -> p j k", k=P)
-        tau = const.tile([P, 8], F32, name="tau")
-        tau2 = const.tile([P, 8], F32, name="tau2")
-        rest = const.tile([P, 8], F32, name="rest")
+        f5 = ftab[:].rearrange("p (g u e k) -> p g u e k", g=2, u=2, e=2)
+        low = const.tile([P, 8], F32, name="low")
+        low4 = low[:].rearrange("p (g u e) -> p g u e", g=2, u=2)
+        low2 = const.tile([P, 8], F32, name="low2")
         sgn = const.tile([P, 1], F32, name="sgn")
         hi = const.tile([P, K], BF16, name="hi")
         ysq = const.tile([P, K], F32, name="ysq")
@@ -92,8 +91,8 @@ def tile_samplinglayer_kernel(tc, x, weight, out):
                 nc.tensor.transpose(tp[:, t * P:(t + 1) * P], ftab[:, j * P:(j + 1) * P], ident_b[:])
             tabps[g] = tp
 
-        def keep_clock_up(n):
-            spare = psum.tile([P, K], F32, tag="pt3", name="spare")
+        def keep_clock_up(n, bank="pt3"):
+            spare = psum.tile([P, K], F32, tag=bank, name="spare")
             for i in range(n):
                 nc.tensor.matmul(out=spare[:], lhsT=idle[:, 0:P], rhs=idle[:], start=True, stop=True)
 
@@ -201,7 +200,8 @@ def tile_samplinglayer_kernel(tc, x, weight, out):
                 xw[t0 + i] = words[:, i * (L // 2):(i + 1) * (L // 2)]
             t0 += n
 
-        nc.gpsimd.iota(tau_i[:], pattern=[[512, 2], [256, 2], [1, 2]], base=1, channel_multiplier=2)
+        nc.gpsimd.iota(low[:], pattern=[[0, 4], [1, 2]], base=1, channel_multiplier=2,
+                       allow_small_or_imprecise_dtypes=True)
         nc.gpsimd.memset(wr[96:126, :].bitcast(U32), 0)
         make_identity(nc, ident_f[:])
         make_identity(nc, ident_b[:])
@@ -214,50 +214,62 @@ def tile_samplinglayer_kernel(tc, x, weight, out):
         nc.scalar.activation(out=warm[:], in_=zero1[:], func=ACT.Exp)
         nc.vector.memset(ftab[:].bitcast(U32), 0)
         nc.vector.memset(f3[:, :, 126:128], 1.0)
-        nc.vector.tensor_copy(out=tau[:], in_=tau_i[:])
-        nc.vector.tensor_tensor(out=tau2[:], in0=tau[:], in1=tau[:], op=ALU.mult)
-        nc.vector.tensor_scalar(out=f3[:, :, 62], in0=tau[:], scalar1=-2.0, scalar2=None, op0=ALU.mult)
-        nc.vector.tensor_copy(out=f3[:, :, 0], in_=tau2[:])
-        nc.vector.scalar_tensor_tensor(out=f3[:, :, 63], in0=tau[:], scalar=-2.0, in1=f3[:, :, 62],
-                                       op0=ALU.mult, op1=ALU.subtract)
-        nc.vector.tensor_tensor(out=rest[:], in0=tau2[:], in1=f3[:, :, 0], op=ALU.subtract)
+        nc.vector.tensor_tensor(out=low2[:], in0=low[:], in1=low[:], op=ALU.mult)
+        nc.vector.tensor_scalar(out=f3[:, :, 62], in0=low[:], scalar1=-2.0, scalar2=None, op0=ALU.mult)
+        for a in range(1, 4):
+            nc.vector.memset(f3[:, 2 * a:2 * a + 2, 63], -512.0 * a)
+        nc.vector.tensor_copy(out=f3[:, :, 0], in_=low2[:])
+        nc.vector.tensor_scalar(out=f5[:, :, 1, :, 2], in0=low4[:, :, 1, :], scalar1=512.0, scalar2=None, op0=ALU.mult)
+        nc.vector.tensor_scalar(out=f5[:, 1, :, :, 3], in0=low4[:, 1, :, :], scalar1=1024.0, scalar2=None, op0=ALU.mult)
+        for a in range(1, 4):
+            nc.vector.memset(f3[:, 2 * a:2 * a + 2, 4], 65536.0 * a * a)
+        nc.vector.tensor_tensor(out=f3[:, :, 1], in0=low2[:], in1=f3[:, :, 0], op=ALU.subtract)
         nc.vector.tensor_tensor(out=sgn[:], in0=ident_f[:, 126:127], in1=ident_f[:, 127:128], op=ALU.subtract)
-        nc.vector.tensor_copy(out=f3[:, :, 1], in_=rest[:])
         nc.vector.tensor_tensor(out=hi[96:128, :], in0=wr[96:128, :], in1=wr[96:128, :], op=ALU.mult)
-        nc.vector.tensor_tensor(out=f3[:, :, 2], in0=rest[:], in1=f3[:, :, 1], op=ALU.subtract)
-
         keep_clock_up(4)
-        transposes(0)
-        transposes(1)
         table_transposes(0)
         table_transposes(1)
-        transposes(2)
-        transposes(3)
-
+        transposes(0)
+        transposes(1)
+        keep_clock_up(1)
         nc.scalar.activation(out=ysq[96:128, :], in_=wr[96:128, :], func=ACT.Square,
                              scale=ident_f[96:128, 127:128])
         nc.vector.scalar_tensor_tensor(out=rhs_w[96:128, :], in0=hi[96:128, :], scalar=sgn[96:128, 0:1],
                                        in1=ysq[96:128, :], op0=ALU.mult, op1=ALU.add)
-        copy_in(0, "S")
         nc.scalar.copy(out=tab[0][:], in_=tabps[0][:])
         nc.scalar.copy(out=tab[1][:], in_=tabps[1][:])
+        copy_in(0, "S")
         copy_in(1, "V")
+        transposes(2)
+        transposes(3)
+        distances(0)
+        distances(1)
+        distances(2)
+        distances(3)
         copy_in(2, "V")
         copy_in(3, "V")
         quantise(0)
-
-        for b in range(4):
-            distances(b)
-        for b in range(4):
-            transposes(b + 4)
-            gauss(b)
-            distances(b + 4)
-        for b in range(4, 8):
-            gauss(b)
+        transposes(4)
+        gauss(0)
+        distances(4)
+        transposes(5)
+        gauss(1)
+        distances(5)
+        transposes(6)
+        gauss(2)
+        distances(6)
+        transposes(7)
+        gauss(3)
+        distances(7)
+        gauss(4)
+        gauss(5)
+        gauss(6)
+        gauss(7)
         copy_in(4, "V")
         transposes(8)
         copy_in(5, "V")
         transposes(9)
+        keep_clock_up(1, "po2")
         quantise_w(0)
         copy_in(6, "V")
         transposes(10)
@@ -265,8 +277,10 @@ def tile_samplinglayer_kernel(tc, x, weight, out):
         transposes(11)
         quantise_w(1)
         quantise(1)
-        for t in range(8, 12):
-            copy_in(t, "S")
+        copy_in(8, "S")
+        copy_in(9, "S")
+        copy_in(10, "S")
+        copy_in(11, "S")
         quantise(2)
         for j in range(8):
             for i in range(4):

@@ -21,6 +21,8 @@ FLOPS = 2 * ROWS * L * K
 LOADS = [1, 1, 1, 1, 2, 2, 4, 4, 4, 4, 4, 4]
 STORES = [4, 4, 4, 4, 4, 2, 2, 2, 2, 1, 1, 1]
 TILES = ROWS // P
+RUNS = 6
+AHEAD = 12
 HALVED = 2
 
 
@@ -113,11 +115,15 @@ def tile_samplinglayer_kernel(tc, x, weight, out):
         def quantise_w(g):
             nc.vector.quantize_mx(out=wcodes[g][:].bitcast(FP8X4), scales=wscl[g][:], in_=wg[g][:])
 
+        def transpose(t, k):
+            if k == 0:
+                bank = psum.tile([P, 512], F32, tag="pt%d" % (t % 4), name="pt_%d" % t)
+                pt[t] = bank
+            nc.tensor.transpose(pt[t][:, k * P:(k + 1) * P], xw[t][:, k * P:(k + 1) * P], ident_f[:])
+
         def transposes(t):
-            bank = psum.tile([P, 512], F32, tag="pt%d" % (t % 4), name="pt_%d" % t)
             for k in range(4):
-                nc.tensor.transpose(bank[:, k * P:(k + 1) * P], xw[t][:, k * P:(k + 1) * P], ident_f[:])
-            pt[t] = bank
+                transpose(t, k)
 
         def copy_in(t, eng):
             j, i = divmod(t, GROUP)
@@ -281,27 +287,41 @@ def tile_samplinglayer_kernel(tc, x, weight, out):
         copy_in(9, "S")
         copy_in(10, "S")
         copy_in(11, "S")
-        quantise(2)
-        for j in range(8):
-            for i in range(4):
-                if 4 * j + i < TILES - HALVED:
-                    mx(4 * j + i, 0)
-                    mx(4 * j + i, 1)
-                else:
-                    mx_half(4 * j + i, 0)
-                    mx_half(4 * j + i, 1)
-            if j + 3 < 8:
-                for i in range(4):
-                    transposes(4 * (j + 3) + i)
-            for i in range(4):
-                on_vector = (i % 2 == 0) if j >= 5 else (i == 0)
-                if 4 * j + i < TILES - HALVED:
-                    copy_out(4 * j + i, "V" if on_vector else "S")
-                else:
-                    copy_half(4 * j + i, 0)
-                    copy_half(4 * j + i, 1)
-            if j >= 1 and j + 2 < 8:
-                quantise(j + 2)
-            if j + 3 < 8:
-                for i in range(4):
-                    copy_in(4 * (j + 3) + i, "V" if i % 2 == 0 else "S")
+        def multiply(t):
+            if t < TILES - HALVED:
+                mx(t, 0)
+                mx(t, 1)
+            else:
+                mx_half(t, 0)
+                mx_half(t, 1)
+
+        def empty(t, eng):
+            if t < TILES - HALVED:
+                copy_out(t, eng)
+            else:
+                copy_half(t, 0)
+                copy_half(t, 1)
+
+        body = TILES - AHEAD
+        ready = 2
+        filled = AHEAD
+        for r in range(RUNS):
+            while GROUP * (ready + 1) <= filled:
+                quantise(ready)
+                ready += 1
+            rows = range(body * r // RUNS, body * (r + 1) // RUNS)
+            for t in rows:
+                multiply(t)
+            for n in range(4 * body * r // RUNS, 4 * body * (r + 1) // RUNS):
+                transpose(AHEAD + n // 4, n % 4)
+            for t in rows:
+                empty(t, "V" if t % 4 == 2 else "S")
+            while filled < AHEAD + 4 * body * (r + 1) // RUNS // 4:
+                copy_in(filled, "S" if filled % 2 else "V")
+                filled += 1
+        quantise(ready)
+        for first in range(body, TILES, GROUP):
+            for t in range(first, first + GROUP):
+                multiply(t)
+            for t in range(first, first + GROUP):
+                empty(t, "V" if t % 4 == 2 or (t % 2 == 0 and first > body) else "S")

@@ -19,7 +19,7 @@ GROUP = 4
 FLOPS = 2 * ROWS * L * K
 
 LOADS = [1, 1, 1, 1, 2, 2, 4, 4, 4, 4, 4, 4]
-STORES = [4, 4, 4, 4, 4, 2, 2, 2, 2, 1, 1, 1]
+STORES = [4, 4, 2, 2, 2, 2, 2, 2, 1, 1, 1, 1, 1, 1, 1, 1, 1, 1, 1]
 TILES = ROWS // P
 RUNS = 6
 AHEAD = 12
@@ -157,7 +157,7 @@ def tile_samplinglayer_kernel(tc, x, weight, out):
         def copy_out(t, eng):
             c, i, n, first = store_of[t]
             if i == 0:
-                ob = opool.tile([P, n * K], F32, tag="ob%d" % n, name="ob_%d" % c, bufs=(3 if n == 4 else 4))
+                ob = opool.tile([P, n * K], F32, tag="ob%d" % n, name="ob_%d" % c, bufs=(3 if n == 4 else 8 if n == 1 else 4))
                 obuf[c] = ob
             dst = obuf[c][:, i * K:(i + 1) * K]
             if eng == "V":
@@ -182,7 +182,7 @@ def tile_samplinglayer_kernel(tc, x, weight, out):
         def copy_half(t, h):
             last = t == TILES - 1
             if h == 0 and not last:
-                obuf[t] = opool.tile([P, K], F32, tag="ob1", name="ob_t%d" % t, bufs=4)
+                obuf[t] = opool.tile([P, K], F32, tag="ob1", name="ob_t%d" % t, bufs=8)
             if last:
                 obuf[t] = opool.tile([P, 256], F32, tag="obh", name="ob_t%d_%d" % (t, h), bufs=2)
             dst = obuf[t][:] if last else obuf[t][:, h * 256:(h + 1) * 256]

@@ -21,7 +21,7 @@ FLOPS = 2 * ROWS * L * K
 LOADS = [1, 1, 1, 1, 2, 2, 4, 4, 4, 4, 4, 4]
 STORES = [4, 4, 2, 2, 2, 2, 2, 2, 1, 1, 1, 1, 1, 1, 1, 1, 1, 1, 1]
 TILES = ROWS // P
-RUNS = 6
+RUNS = 5
 AHEAD = 12
 HALVED = 2
 

from contextlib import ExitStack

import concourse.mybir as mybir
from concourse.masks import make_identity

F32 = mybir.dt.float32
BF16 = mybir.dt.bfloat16
U32 = mybir.dt.uint32
U8 = mybir.dt.uint8
FP8X4 = mybir.dt.float8_e4m3fn_x4
ACT = mybir.ActivationFunctionType
ALU = mybir.AluOpType

P = 128
ROWS = 4096
L = 1024
K = 512
GROUP = 4
FLOPS = 2 * ROWS * L * K

LOADS = [1, 1, 1, 1, 2, 2, 4, 4, 4, 4, 4, 4]
STORES = [4, 4, 2, 2, 2, 2, 2, 2, 1, 1, 1, 1, 1, 1, 1, 1, 1, 1, 1]
TILES = ROWS // P
RUNS = 5
AHEAD = 12
HALVED = 2


def tile_samplinglayer_kernel(tc, x, weight, out):
    nc = tc.nc
    xv = x.rearrange("(p a) f -> p (a f)", p=P)
    ov = out.rearrange("(p a) f -> p (a f)", p=P)

    with ExitStack() as ctx:
        const = ctx.enter_context(tc.tile_pool(name="const", bufs=1))
        xpool = ctx.enter_context(tc.tile_pool(name="xpool", bufs=1))
        gpool = ctx.enter_context(tc.tile_pool(name="gpool", bufs=4))
        cpool = ctx.enter_context(tc.tile_pool(name="cpool", bufs=1))
        opool = ctx.enter_context(tc.tile_pool(name="opool", bufs=3))
        psum = ctx.enter_context(tc.psum_pool(name="psum", bufs=1))
        ctx.enter_context(tc.manual_schedule())

        wr = const.tile([P, K], BF16, name="wr")
        rhs_w = const.tile([P, K], BF16, name="rhs_w")
        ident_f = const.tile([P, P], F32, name="ident_f")
        ident_b = const.tile([P, P], BF16, name="ident_b")
        zero1 = const.tile([P, 1], F32, name="zero1")
        idle = const.tile([P, K], BF16, name="idle")
        warm = const.tile([P, 1], F32, name="warm")
        ftab = const.tile([P, 8 * P], BF16, name="ftab")
        f3 = ftab[:].rearrange("p (j k) -> p j k", k=P)
        f5 = ftab[:].rearrange("p (g u e k) -> p g u e k", g=2, u=2, e=2)
        low = const.tile([P, 8], F32, name="low")
        low4 = low[:].rearrange("p (g u e) -> p g u e", g=2, u=2)
        low2 = const.tile([P, 8], F32, name="low2")
        sgn = const.tile([P, 1], F32, name="sgn")
        hi = const.tile([P, K], BF16, name="hi")
        ysq = const.tile([P, K], F32, name="ysq")
        tab = []
        wg = []
        wcodes = []
        wscl = []
        for g in range(2):
            tb = const.tile([P, 4 * P], BF16, name="tab%d" % g)
            wg_g = const.tile([P, 4 * K], BF16, name="wg%d" % g, align_bytes=64)
            wc_g = const.tile([P, K], U32, name="wcodes%d" % g, align_bytes=64)
            ws_g = const.tile([P, K], U8, name="wscl%d" % g, align_bytes=64)
            tab.append(tb)
            wg.append(wg_g)
            wcodes.append(wc_g)
            wscl.append(ws_g)

        xw = {}
        tabps = {}
        wbank = {}
        pt = {}
        po = {}
        grouped = {}
        codes = {}
        scales = {}
        obuf = {}
        store_of = {}
        t0 = 0
        for c, n in enumerate(STORES):
            for i in range(n):
                store_of[t0 + i] = (c, i, n, t0)
            t0 += n

        def table_transposes(g):
            tp = psum.tile([P, 4 * P], BF16, tag="po%d" % g, name="tabps%d" % g)
            for t in range(4):
                j = 4 * g + t
                nc.tensor.transpose(tp[:, t * P:(t + 1) * P], ftab[:, j * P:(j + 1) * P], ident_b[:])
            tabps[g] = tp

        def keep_clock_up(n, bank="pt3"):
            spare = psum.tile([P, K], F32, tag=bank, name="spare")
            for i in range(n):
                nc.tensor.matmul(out=spare[:], lhsT=idle[:, 0:P], rhs=idle[:], start=True, stop=True)

        def distances(b):
            g, nb = divmod(b, 4)
            bank = psum.tile([P, 512], F32, tag="po%d" % ((b + 2) % 4), name="wd%d" % b)
            for t in range(4):
                nc.tensor.matmul(out=bank[:, t * P:(t + 1) * P], lhsT=tab[g][:, t * P:(t + 1) * P],
                                 rhs=rhs_w[:, nb * P:(nb + 1) * P], start=True, stop=True)
            wbank[b] = bank

        def gauss(b):
            g, nb = divmod(b, 4)
            grouped_w = wg[g][:, nb * 512:(nb + 1) * 512].rearrange("p (n t) -> p n t", t=4)
            nc.scalar.activation(out=grouped_w, in_=wbank[b][:].rearrange("p (t n) -> p n t", t=4), func=ACT.Exp,
                                 scale=-0.01)

        def quantise_w(g):
            nc.vector.quantize_mx(out=wcodes[g][:].bitcast(FP8X4), scales=wscl[g][:], in_=wg[g][:])

        def transpose(t, k):
            if k == 0:
                bank = psum.tile([P, 512], F32, tag="pt%d" % (t % 4), name="pt_%d" % t)
                pt[t] = bank
            nc.tensor.transpose(pt[t][:, k * P:(k + 1) * P], xw[t][:, k * P:(k + 1) * P], ident_f[:])

        def transposes(t):
            for k in range(4):
                transpose(t, k)

        def copy_in(t, eng):
            j, i = divmod(t, GROUP)
            if i == 0:
                gr = gpool.tile([P, GROUP * L], BF16, tag="gr", name="gr%d" % j, align_bytes=64)
                grouped[j] = gr
            dst = grouped[j][:].bitcast(F32)[:, i * 512:(i + 1) * 512].rearrange("p (g m u) -> p g m u", g=2, u=2)
            src = pt[t][:].rearrange("p (g u m) -> p g m u", g=2, u=2)
            if eng == "V":
                nc.vector.tensor_copy(out=dst, in_=src)
            else:
                nc.scalar.copy(out=dst, in_=src)

        def quantise(j):
            cj = cpool.tile([P, GROUP * 256], U32, name="codes%d" % j, align_bytes=64)
            sj = cpool.tile([P, GROUP * 256], U8, name="scales%d" % j, align_bytes=64)
            nc.vector.quantize_mx(out=cj[:].bitcast(FP8X4), scales=sj[:], in_=grouped[j][:])
            codes[j] = cj
            scales[j] = sj

        def mx(t, g):
            j, i = divmod(t, GROUP)
            if g == 0:
                acc = psum.tile([P, K], F32, tag="po%d" % (t % 4), name="po_%d" % t)
                po[t] = acc
            cols = slice(i * 256 + g * P, i * 256 + (g + 1) * P)
            nc.tensor.matmul_mx(out=po[t][:], lhsT=codes[j][:, cols].bitcast(FP8X4), lhsT_scale=scales[j][:, cols],
                                rhs=wcodes[g][:].bitcast(FP8X4), rhs_scale=wscl[g][:],
                                start=(g == 0), stop=(g == 1))

        def copy_out(t, eng):
            c, i, n, first = store_of[t]
            if i == 0:
                ob = opool.tile([P, n * K], F32, tag="ob%d" % n, name="ob_%d" % c, bufs=(3 if n == 4 else 8 if n == 1 else 4))
                obuf[c] = ob
            dst = obuf[c][:, i * K:(i + 1) * K]
            if eng == "V":
                nc.vector.tensor_copy(out=dst, in_=po[t][:])
            else:
                nc.scalar.copy(out=dst, in_=po[t][:])
            if i == n - 1:
                nc.sync.dma_start(out=ov[:, first * K:(first + n) * K], in_=obuf[c][:])

        def mx_half(t, h):
            j, i = divmod(t, GROUP)
            acc = psum.tile([P, K], F32, tag=("po%d" if h == 0 else "pt%d") % (t % 4), name="po_%d_%d" % (t, h))
            po[t, h] = acc
            for g in range(2):
                cols = slice(i * 256 + g * P, i * 256 + (g + 1) * P)
                half = slice(h * 256, (h + 1) * 256)
                nc.tensor.matmul_mx(out=acc[:, 0:256], lhsT=codes[j][:, cols].bitcast(FP8X4),
                                    lhsT_scale=scales[j][:, cols],
                                    rhs=wcodes[g][:, half].bitcast(FP8X4), rhs_scale=wscl[g][:, half],
                                    start=(g == 0), stop=(g == 1))

        def copy_half(t, h):
            last = t == TILES - 1
            if h == 0 and not last:
                obuf[t] = opool.tile([P, K], F32, tag="ob1", name="ob_t%d" % t, bufs=8)
            if last:
                obuf[t] = opool.tile([P, 256], F32, tag="obh", name="ob_t%d_%d" % (t, h), bufs=2)
            dst = obuf[t][:] if last else obuf[t][:, h * 256:(h + 1) * 256]
            if h == 0:
                nc.vector.tensor_copy(out=dst, in_=po[t, h][:, 0:256])
            else:
                nc.scalar.copy(out=dst, in_=po[t, h][:, 0:256])
            if last:
                nc.sync.dma_start(out=ov[:, t * K + h * 256:t * K + (h + 1) * 256], in_=obuf[t][:])
            elif h == 1:
                nc.sync.dma_start(out=ov[:, t * K:(t + 1) * K], in_=obuf[t][:])

        nc.sync.dma_start(out=wr[126:128, :], in_=weight.partition_broadcast(2))
        nc.sync.dma_start(out=rhs_w[62:64, :], in_=weight.partition_broadcast(2))
        t0 = 0
        for c, n in enumerate(LOADS):
            xt = xpool.tile([P, n * L], BF16, name="x%d" % c)
            nc.sync.dma_start(out=xt[:], in_=xv[:, t0 * L:(t0 + n) * L])
            words = xt[:].bitcast(F32)
            for i in range(n):
                xw[t0 + i] = words[:, i * (L // 2):(i + 1) * (L // 2)]
            t0 += n

        nc.gpsimd.iota(low[:], pattern=[[0, 4], [1, 2]], base=1, channel_multiplier=2,
                       allow_small_or_imprecise_dtypes=True)
        nc.gpsimd.memset(wr[96:126, :].bitcast(U32), 0)
        make_identity(nc, ident_f[:])
        make_identity(nc, ident_b[:])
        nc.gpsimd.memset(rhs_w[0:32, :], 1.0)
        nc.gpsimd.memset(rhs_w[32:62, :].bitcast(U32), 0)
        nc.gpsimd.memset(rhs_w[64:96, :].bitcast(U32), 0)

        nc.vector.memset(zero1[:], 0.0)
        nc.vector.memset(idle[:].bitcast(U32), 0)
        nc.scalar.activation(out=warm[:], in_=zero1[:], func=ACT.Exp)
        nc.vector.memset(ftab[:].bitcast(U32), 0)
        nc.vector.memset(f3[:, :, 126:128], 1.0)
        nc.vector.tensor_tensor(out=low2[:], in0=low[:], in1=low[:], op=ALU.mult)
        nc.vector.tensor_scalar(out=f3[:, :, 62], in0=low[:], scalar1=-2.0, scalar2=None, op0=ALU.mult)
        for a in range(1, 4):
            nc.vector.memset(f3[:, 2 * a:2 * a + 2, 63], -512.0 * a)
        nc.vector.tensor_copy(out=f3[:, :, 0], in_=low2[:])
        nc.vector.tensor_scalar(out=f5[:, :, 1, :, 2], in0=low4[:, :, 1, :], scalar1=512.0, scalar2=None, op0=ALU.mult)
        nc.vector.tensor_scalar(out=f5[:, 1, :, :, 3], in0=low4[:, 1, :, :], scalar1=1024.0, scalar2=None, op0=ALU.mult)
        for a in range(1, 4):
            nc.vector.memset(f3[:, 2 * a:2 * a + 2, 4], 65536.0 * a * a)
        nc.vector.tensor_tensor(out=f3[:, :, 1], in0=low2[:], in1=f3[:, :, 0], op=ALU.subtract)
        nc.vector.tensor_tensor(out=sgn[:], in0=ident_f[:, 126:127], in1=ident_f[:, 127:128], op=ALU.subtract)
        nc.vector.tensor_tensor(out=hi[96:128, :], in0=wr[96:128, :], in1=wr[96:128, :], op=ALU.mult)
        keep_clock_up(4)
        table_transposes(0)
        table_transposes(1)
        transposes(0)
        transposes(1)
        keep_clock_up(1)
        nc.scalar.activation(out=ysq[96:128, :], in_=wr[96:128, :], func=ACT.Square,
                             scale=ident_f[96:128, 127:128])
        nc.vector.scalar_tensor_tensor(out=rhs_w[96:128, :], in0=hi[96:128, :], scalar=sgn[96:128, 0:1],
                                       in1=ysq[96:128, :], op0=ALU.mult, op1=ALU.add)
        nc.scalar.copy(out=tab[0][:], in_=tabps[0][:])
        nc.scalar.copy(out=tab[1][:], in_=tabps[1][:])
        copy_in(0, "S")
        copy_in(1, "V")
        transposes(2)
        transposes(3)
        distances(0)
        distances(1)
        distances(2)
        distances(3)
        copy_in(2, "V")
        copy_in(3, "V")
        quantise(0)
        transposes(4)
        gauss(0)
        distances(4)
        transposes(5)
        gauss(1)
        distances(5)
        transposes(6)
        gauss(2)
        distances(6)
        transposes(7)
        gauss(3)
        distances(7)
        gauss(4)
        gauss(5)
        gauss(6)
        gauss(7)
        copy_in(4, "V")
        transposes(8)
        copy_in(5, "V")
        transposes(9)
        keep_clock_up(1, "po2")
        quantise_w(0)
        copy_in(6, "V")
        transposes(10)
        copy_in(7, "V")
        transposes(11)
        quantise_w(1)
        quantise(1)
        copy_in(8, "S")
        copy_in(9, "S")
        copy_in(10, "S")
        copy_in(11, "S")
        def multiply(t):
            if t < TILES - HALVED:
                mx(t, 0)
                mx(t, 1)
            else:
                mx_half(t, 0)
                mx_half(t, 1)

        def empty(t, eng):
            if t < TILES - HALVED:
                copy_out(t, eng)
            else:
                copy_half(t, 0)
                copy_half(t, 1)

        body = TILES - AHEAD
        ready = 2
        filled = AHEAD
        for r in range(RUNS):
            while GROUP * (ready + 1) <= filled:
                quantise(ready)
                ready += 1
            rows = range(body * r // RUNS, body * (r + 1) // RUNS)
            for t in rows:
                multiply(t)
            for n in range(4 * body * r // RUNS, 4 * body * (r + 1) // RUNS):
                transpose(AHEAD + n // 4, n % 4)
            for t in rows:
                empty(t, "V" if t % 4 == 2 else "S")
            while filled < AHEAD + 4 * body * (r + 1) // RUNS // 4:
                copy_in(filled, "S" if filled % 2 else "V")
                filled += 1
        quantise(ready)
        for first in range(body, TILES, GROUP):
            for t in range(first, first + GROUP):
                multiply(t)
            for t in range(first, first + GROUP):
                empty(t, "V" if t % 4 == 2 or (t % 2 == 0 and first > body) else "S")
